import numpy as np
import ml_dtypes


BF16 = ml_dtypes.bfloat16


def bf(x):
    return np.asarray(x, np.float32).astype(BF16)


def f64(x):
    return np.asarray(x).astype(np.float64)


E2M1 = np.array([0.0, 0.5, 1.0, 1.5, 2.0, 3.0, 4.0, 6.0, -0.0, -0.5, -1.0, -1.5, -2.0, -3.0, -4.0, -6.0])


def pack_weight(w, fmt):
    k, n = w.shape
    w = f64(bf(w)).reshape(k // 32, 32, n)
    amax = np.abs(w).max(1)
    if fmt == "e4m3":
        byte = np.frexp(amax)[1] - 1 + 127 - 7
    else:
        mant, ex = np.frexp(amax / 6.0)
        byte = np.where(mant > 0.5, ex, ex - 1) + 127
    byte = np.clip(np.where(amax > 0, byte, 1), 1, 254)
    scaled = (w * np.exp2(127.0 - byte)[:, None, :]).reshape(k, n).astype(np.float32)
    by_word = np.ascontiguousarray(scaled.reshape(k // 512, 128, 4, n).transpose(0, 1, 3, 2))
    if fmt == "e4m3":
        words = by_word.astype(ml_dtypes.float8_e4m3fn).view(np.uint8)
    else:
        c = by_word.astype(ml_dtypes.float4_e2m1fn).view(np.uint8) & 0xF
        words = c[..., 0::2] | (c[..., 1::2] << 4)
    return np.ascontiguousarray(words), np.ascontiguousarray(byte.astype(np.uint8).reshape(k // 512, 16, n))


def unpack_weight(words, scales, fmt):
    g, p, n, _ = words.shape
    if fmt == "e4m3":
        vals = np.ascontiguousarray(words).view(ml_dtypes.float8_e4m3fn).astype(np.float64)
    else:
        nib = np.empty((g, p, n, 4), np.uint8)
        nib[..., 0::2] = words & 0xF
        nib[..., 1::2] = words >> 4
        vals = E2M1[nib]
    vals = vals * np.repeat(np.exp2(scales.astype(np.float64) - 127.0), 8, axis=1)[..., None]
    return vals.transpose(0, 1, 3, 2).reshape(g * 512, n)

def pack4(w):
    words, scales = pack_weight(w, "e2m1")
    return words.reshape(words.shape[0], 128, -1), scales


def unpack4(words, scales):
    return unpack_weight(words.reshape(words.shape[0], 128, -1, 2), scales, "e2m1")


def kspread(k):
    return np.exp2(np.repeat(np.random.randint(-6, 7, k // 32), 32).astype(np.float64))


S, D, H, DH = 512, 1536, 16, 128
ROPE_BASE = 10000.0


def rotate_half(v):
    shp = v.shape
    p = v.reshape(*shp[:-1], shp[-1] // 2, 2)
    return np.stack((-p[..., 1], p[..., 0]), axis=-1).reshape(shp)


def rope_cos_sin(seq_len, dh):
    inv_freq = 1.0 / (ROPE_BASE ** (np.arange(0, dh, 2) / dh))
    t = np.arange(seq_len)
    freqs = t[:, None] * inv_freq[None, :]
    return np.repeat(np.cos(freqs), 2, axis=-1), np.repeat(np.sin(freqs), 2, axis=-1)


def setup_inputs():
    s = kspread(D)
    x = np.random.standard_normal((S, D)) * s
    x_words, x_scales = pack4(np.ascontiguousarray(x.T))
    w = np.random.standard_normal((H * DH, D)) / np.sqrt(D) / s[None, :]
    words, scales = pack4(np.ascontiguousarray(w.T))
    return {"x_words": x_words, "x_scales": x_scales, "w_words": words, "w_scales": scales}


def reference(x_words, x_scales, w_words, w_scales):
    y = unpack4(x_words, x_scales).T @ unpack4(w_words, w_scales)
    q = y.reshape(S, H, DH).transpose(1, 0, 2)
    cos, sin = rope_cos_sin(S, DH)
    return q * cos[None] + rotate_half(q) * sin[None]

@@ -1,0 +1,180 @@
+import math
+from contextlib import ExitStack
+
+import concourse.mybir as mybir
+
+S, D, H, DH = 512, 1536, 16, 128
+G = D // 512
+ROPE_BASE = 10000.0
+FLOPS = 2 * S * D * H * DH
+
+F32 = mybir.dt.float32
+BF16 = mybir.dt.bfloat16
+I32 = mybir.dt.int32
+U8 = mybir.dt.uint8
+FP4 = mybir.dt.float4_e2m1fn_x4
+ALU = mybir.AluOpType
+SIN = mybir.ActivationFunctionType.Sin
+
+P = 128
+NB = S // P
+CB = 512
+NC = H * DH // CB
+HB = CB // DH
+J = DH // 2
+TWO_PI = 2.0 * math.pi
+WARM = 8
+
+
+def tile_attention_pa_kernel(tc, x_words, x_scales, w_words, w_scales, out):
+    nc = tc.nc
+    with ExitStack() as ctx:
+        keep = ctx.enter_context(tc.tile_pool(name="keep", bufs=1))
+        work = ctx.enter_context(tc.tile_pool(name="work", bufs=1))
+        psum = ctx.enter_context(tc.psum_pool(name="psum", bufs=8))
+        ctx.enter_context(tc.manual_schedule())
+
+        x0 = keep.tile([P, G, 2 * P], U8, align_bytes=64)
+        xr = keep.tile([P, G, 2 * (S - P)], U8, align_bytes=64)
+        xs = keep.tile([P, G, S], U8, align_bytes=64)
+        w0 = [keep.tile([P, 2 * CB], U8, name="w0_%d" % g, align_bytes=64) for g in range(G)]
+        wr = [keep.tile([P, G, 2 * CB], U8, name="w_%d" % c, align_bytes=64) for c in range(1, NC)]
+        ws0 = keep.tile([P, G, CB], U8, align_bytes=64)
+        wsr = keep.tile([P, G, (NC - 1) * CB], U8, align_bytes=64)
+
+        zeros = keep.tile([P, CB], BF16, align_bytes=64)
+        pos = keep.tile([P, NB], F32)
+        freq = keep.tile([P, J], F32)
+        turns = keep.tile([P, 2, NB, J], F32)
+        whole = keep.tile([P, 2, NB, J], I32)
+        frac = keep.tile([P, 2, NB, J], F32)
+        dummy = keep.tile([P, 1], F32)
+        dummy2 = keep.tile([P, 1], F32)
+        coef = [keep.tile([P, 2, DH], F32, name="coef_%d" % b) for b in range(NB)]
+
+        nc.vector.memset(xs[:].rearrange("p g n -> p (g n)").bitcast(I32), 0)
+        nc.vector.memset(ws0[:].rearrange("p g n -> p (g n)").bitcast(I32), 0)
+        nc.vector.memset(dummy[:], 0.0)
+        nc.gpsimd.memset(zeros[:], 0.0)
+        nc.gpsimd.iota(pos[:], pattern=[[P, NB]], base=0, channel_multiplier=1, allow_small_or_imprecise_dtypes=True)
+        nc.gpsimd.memset(wsr[:].rearrange("p g n -> p (g n)").bitcast(I32), 0)
+        nc.scalar.activation(out=dummy2[:], in_=dummy[:], func=SIN)
+
+        def load_codes(dst, src):
+            nc.sync.dma_start(out=dst.bitcast(I32), in_=src.bitcast(I32))
+
+        def load_scales(dst, src):
+            for q in range(4):
+                nc.sync.dma_start(
+                    out=dst[32 * q : 32 * q + 4, :, :].bitcast(I32),
+                    in_=src[:, 4 * q : 4 * q + 4, :].rearrange("g r n -> r g n").bitcast(I32),
+                )
+
+        load_codes(x0[:], x_words[:, :, 0 : 2 * P].rearrange("g p c -> p g c"))
+        load_codes(w0[0][:], w_words[0, :, 0 : 2 * CB])
+        load_scales(xs, x_scales)
+        load_scales(ws0, w_scales[:, :, 0:CB])
+        load_codes(w0[1][:], w_words[1, :, 0 : 2 * CB])
+        load_codes(w0[2][:], w_words[2, :, 0 : 2 * CB])
+        load_codes(xr[:], x_words[:, :, 2 * P :].rearrange("g p c -> p g c"))
+        load_codes(wr[0][:], w_words[:, :, 2 * CB : 4 * CB].rearrange("g p c -> p g c"))
+        load_scales(wsr, w_scales[:, :, CB:])
+        load_codes(wr[1][:], w_words[:, :, 4 * CB : 6 * CB].rearrange("g p c -> p g c"))
+        load_codes(wr[2][:], w_words[:, :, 6 * CB : 8 * CB].rearrange("g p c -> p g c"))
+
+        warm = psum.tile([P, CB], F32, name="acc", tag="acc")
+        for i in range(WARM):
+            nc.tensor.matmul(warm[:], lhsT=zeros[:, 0:P], rhs=zeros[:], start=True, stop=True)
+
+        nc.vector.memset(freq[:, 0:1], 1.0)
+        n = 1
+        while n < J:
+            nc.vector.tensor_scalar_mul(freq[:, n : 2 * n], freq[:, 0:n], ROPE_BASE ** (-n / J))
+            n *= 2
+        nc.vector.scalar_tensor_tensor(
+            out=turns[:, 1, :, :],
+            in0=pos[:].unsqueeze(2).to_broadcast([P, NB, J]),
+            scalar=1.0 / TWO_PI,
+            in1=freq[:].unsqueeze(1).to_broadcast([P, NB, J]),
+            op0=ALU.mult,
+            op1=ALU.mult,
+        )
+        nc.vector.tensor_scalar_add(turns[:, 0, :, :], turns[:, 1, :, :], 0.25)
+        nc.vector.tensor_copy(out=whole[:], in_=turns[:])
+        nc.vector.tensor_tensor(out=frac[:], in0=turns[:], in1=whole[:], op=ALU.subtract)
+        for b in range(NB):
+            nc.scalar.activation(
+                out=coef[b][:, 0, :].rearrange("p (j e) -> p j e", e=2),
+                in_=frac[:, 0, b, :].unsqueeze(2).to_broadcast([P, J, 2]),
+                func=SIN,
+                scale=TWO_PI,
+            )
+            for e in range(2):
+                nc.scalar.activation(
+                    out=coef[b][:, 1, e::2],
+                    in_=frac[:, 1, b, :],
+                    func=SIN,
+                    scale=TWO_PI if e == 0 else -TWO_PI,
+                )
+
+        def codes(c, b, g, lo, hi):
+            if b == 0:
+                lhs = x0[:, g, :]
+            else:
+                lhs = xr[:, g, 2 * P * (b - 1) : 2 * P * b]
+            if c == 0:
+                rhs, scale = w0[g][:, 2 * lo : 2 * hi], ws0[:, g, lo:hi]
+            else:
+                rhs = wr[c - 1][:, g, 2 * lo : 2 * hi]
+                scale = wsr[:, g, CB * (c - 1) + lo : CB * (c - 1) + hi]
+            return lhs.bitcast(FP4), xs[:, g, P * b : P * (b + 1)], rhs.bitcast(FP4), scale
+
+        def multiply(c, b, lo, hi):
+            acc = psum.tile([P, CB], F32, name="acc", tag="acc")
+            for g in range(G):
+                lhs, ls, rhs, rs = codes(c, b, g, lo, hi)
+                nc.tensor.matmul_mx(
+                    out=acc[:, 0 : hi - lo], lhsT=lhs, lhsT_scale=ls, rhs=rhs, rhs_scale=rs, start=(g == 0), stop=(g == G - 1)
+                )
+            return acc
+
+        def products(acc, b, n):
+            prod = work.tile([P, 2, CB], F32, name="prod", tag="prod", bufs=8)
+            h = n // DH
+            nc.vector.tensor_tensor(
+                out=prod[:, :, 0:n].rearrange("p t (h c) -> p t h c", h=h),
+                in0=acc[:, 0:n].rearrange("p (h c) -> p h c", h=h).unsqueeze(1).to_broadcast([P, 2, h, DH]),
+                in1=coef[b][:].unsqueeze(2).to_broadcast([P, 2, h, DH]),
+                op=ALU.mult,
+            )
+            return prod
+
+        def add_store(engine, prod, c, b, lo, hi):
+            n = hi - lo
+            res = work.tile([P, CB], F32, name="res", tag="res", bufs=8)
+            engine.tensor_tensor(
+                out=res[:, 0:n].rearrange("p (j e) -> p j e", e=2),
+                in0=prod[:, 0, 0:n].rearrange("p (j e) -> p j e", e=2),
+                in1=prod[:, 1, 0:n].rearrange("p (j e) -> p j e", e=2)[:, :, ::-1],
+                op=ALU.add,
+            )
+            h0 = HB * c + lo // DH
+            nc.sync.dma_start(
+                out=out[h0 : h0 + n // DH, P * b : P * (b + 1), :].rearrange("h p d -> p h d"),
+                in_=res[:, 0:n].rearrange("p (h d) -> p h d", d=DH),
+            )
+
+        items = []
+        for c in range(NC):
+            for b in range(NB):
+                first = c == 0 and b == 0
+                last = c == NC - 1 and b == NB - 1
+                if first or last:
+                    items.append((c, b, 0, CB // 2, last))
+                    items.append((c, b, CB // 2, CB, last))
+                else:
+                    items.append((c, b, 0, CB, False))
+        for c, b, lo, hi, on_vector in items:
+            acc = multiply(c, b, lo, hi)
+            prod = products(acc, b, hi - lo)
+            add_store(nc.vector if on_vector else nc.gpsimd, prod, c, b, lo, hi)

@@ -2,6 +2,7 @@ import math
 from contextlib import ExitStack
 
 import concourse.mybir as mybir
+from concourse.masks import make_identity
 
 S, D, H, DH = 512, 1536, 16, 128
 G = D // 512
@@ -24,6 +25,7 @@ HB = CB // DH
 J = DH // 2
 TWO_PI = 2.0 * math.pi
 WARM = 8
+MODES = ["GG","G","G","G","G","G","A","B","A","B","A","B","C","G","G","VV"]
 
 
 def tile_attention_pa_kernel(tc, x_words, x_scales, w_words, w_scales, out):
@@ -43,21 +45,21 @@ def tile_attention_pa_kernel(tc, x_words, x_scales, w_words, w_scales, out):
         wsr = keep.tile([P, G, (NC - 1) * CB], U8, align_bytes=64)
 
         zeros = keep.tile([P, CB], BF16, align_bytes=64)
+        ident = keep.tile([P, P], F32, align_bytes=64)
         pos = keep.tile([P, NB], F32)
         freq = keep.tile([P, J], F32)
-        turns = keep.tile([P, 2, NB, J], F32)
-        whole = keep.tile([P, 2, NB, J], I32)
-        frac = keep.tile([P, 2, NB, J], F32)
         dummy = keep.tile([P, 1], F32)
         dummy2 = keep.tile([P, 1], F32)
         coef = [keep.tile([P, 2, DH], F32, name="coef_%d" % b) for b in range(NB)]
 
         nc.vector.memset(xs[:].rearrange("p g n -> p (g n)").bitcast(I32), 0)
-        nc.vector.memset(ws0[:].rearrange("p g n -> p (g n)").bitcast(I32), 0)
         nc.vector.memset(dummy[:], 0.0)
-        nc.gpsimd.memset(zeros[:], 0.0)
+        nc.vector.memset(freq[:, 0:1], 1.0)
+        nc.vector.memset(ws0[:].rearrange("p g n -> p (g n)").bitcast(I32), 0)
         nc.gpsimd.iota(pos[:], pattern=[[P, NB]], base=0, channel_multiplier=1, allow_small_or_imprecise_dtypes=True)
+        nc.gpsimd.memset(zeros[:], 0.0)
         nc.gpsimd.memset(wsr[:].rearrange("p g n -> p (g n)").bitcast(I32), 0)
+        make_identity(nc, ident[:])
         nc.scalar.activation(out=dummy2[:], in_=dummy[:], func=SIN)
 
         def load_codes(dst, src):
@@ -86,36 +88,47 @@ def tile_attention_pa_kernel(tc, x_words, x_scales, w_words, w_scales, out):
         for i in range(WARM):
             nc.tensor.matmul(warm[:], lhsT=zeros[:, 0:P], rhs=zeros[:], start=True, stop=True)
 
-        nc.vector.memset(freq[:, 0:1], 1.0)
         n = 1
         while n < J:
             nc.vector.tensor_scalar_mul(freq[:, n : 2 * n], freq[:, 0:n], ROPE_BASE ** (-n / J))
             n *= 2
-        nc.vector.scalar_tensor_tensor(
-            out=turns[:, 1, :, :],
-            in0=pos[:].unsqueeze(2).to_broadcast([P, NB, J]),
-            scalar=1.0 / TWO_PI,
-            in1=freq[:].unsqueeze(1).to_broadcast([P, NB, J]),
-            op0=ALU.mult,
-            op1=ALU.mult,
-        )
-        nc.vector.tensor_scalar_add(turns[:, 0, :, :], turns[:, 1, :, :], 0.25)
-        nc.vector.tensor_copy(out=whole[:], in_=turns[:])
-        nc.vector.tensor_tensor(out=frac[:], in0=turns[:], in1=whole[:], op=ALU.subtract)
-        for b in range(NB):
-            nc.scalar.activation(
-                out=coef[b][:, 0, :].rearrange("p (j e) -> p j e", e=2),
-                in_=frac[:, 0, b, :].unsqueeze(2).to_broadcast([P, J, 2]),
-                func=SIN,
-                scale=TWO_PI,
-            )
-            for e in range(2):
+
+        def tables(b0, b1):
+            m = b1 - b0
+            turns = keep.tile([P, 2, m, J], F32, name="turns_%d" % b0)
+            whole = keep.tile([P, 2, m, J], I32, name="whole_%d" % b0)
+            frac = keep.tile([P, 2, m, J], F32, name="frac_%d" % b0)
+            for t, quarter in ((1, 0.0), (0, 0.25)):
+                if t == 1:
+                    nc.vector.scalar_tensor_tensor(
+                        out=turns[:, 1, :, :],
+                        in0=pos[:, b0:b1].unsqueeze(2).to_broadcast([P, m, J]),
+                        scalar=1.0 / TWO_PI,
+                        in1=freq[:].unsqueeze(1).to_broadcast([P, m, J]),
+                        op0=ALU.mult,
+                        op1=ALU.mult,
+                    )
+                else:
+                    nc.vector.tensor_scalar_add(turns[:, 0, :, :], turns[:, 1, :, :], quarter)
+            nc.vector.tensor_copy(out=whole[:], in_=turns[:])
+            nc.vector.tensor_tensor(out=frac[:], in0=turns[:], in1=whole[:], op=ALU.subtract)
+            for b in range(b0, b1):
                 nc.scalar.activation(
-                    out=coef[b][:, 1, e::2],
-                    in_=frac[:, 1, b, :],
+                    out=coef[b][:, 0, :].rearrange("p (j e) -> p j e", e=2),
+                    in_=frac[:, 0, b - b0, :].unsqueeze(2).to_broadcast([P, J, 2]),
                     func=SIN,
-                    scale=TWO_PI if e == 0 else -TWO_PI,
+                    scale=TWO_PI,
                 )
+                for e in range(2):
+                    nc.scalar.activation(
+                        out=coef[b][:, 1, e::2],
+                        in_=frac[:, 1, b - b0, :],
+                        func=SIN,
+                        scale=TWO_PI if e == 0 else -TWO_PI,
+                    )
+
+        tables(0, 1)
+        tables(1, NB)
 
         def codes(c, b, g, lo, hi):
             if b == 0:
@@ -138,43 +151,99 @@ def tile_attention_pa_kernel(tc, x_words, x_scales, w_words, w_scales, out):
                 )
             return acc
 
-        def products(acc, b, n):
-            prod = work.tile([P, 2, CB], F32, name="prod", tag="prod", bufs=8)
+        def pairs(ap):
+            return ap.rearrange("p (j e) -> p j e", e=2)
+
+        def products(acc, b, n, prod):
             h = n // DH
             nc.vector.tensor_tensor(
-                out=prod[:, :, 0:n].rearrange("p t (h c) -> p t h c", h=h),
+                out=prod.rearrange("p t (h c) -> p t h c", h=h),
                 in0=acc[:, 0:n].rearrange("p (h c) -> p h c", h=h).unsqueeze(1).to_broadcast([P, 2, h, DH]),
                 in1=coef[b][:].unsqueeze(2).to_broadcast([P, 2, h, DH]),
                 op=ALU.mult,
             )
-            return prod
 
-        def add_store(engine, prod, c, b, lo, hi):
-            n = hi - lo
-            res = work.tile([P, CB], F32, name="res", tag="res", bufs=8)
-            engine.tensor_tensor(
-                out=res[:, 0:n].rearrange("p (j e) -> p j e", e=2),
-                in0=prod[:, 0, 0:n].rearrange("p (j e) -> p j e", e=2),
-                in1=prod[:, 1, 0:n].rearrange("p (j e) -> p j e", e=2)[:, :, ::-1],
-                op=ALU.add,
+        def straight_product(prod, acc, b):
+            nc.vector.tensor_tensor(
+                out=prod[:, 0, :].rearrange("p (h c) -> p h c", h=HB),
+                in0=acc[:].rearrange("p (h c) -> p h c", h=HB),
+                in1=coef[b][:, 0, :].unsqueeze(1).to_broadcast([P, HB, DH]),
+                op=ALU.mult,
             )
+
+        def rotated_product(engine, prod, y, b):
+            engine.tensor_tensor(
+                out=prod[:, 1, :].rearrange("p (h j e) -> p h j e", h=HB, e=2),
+                in0=y[:].rearrange("p (h j e) -> p h j e", h=HB, e=2)[:, :, :, ::-1],
+                in1=pairs(coef[b][:, 1, :])[:, :, ::-1].unsqueeze(1).to_broadcast([P, HB, J, 2]),
+                op=ALU.mult,
+            )
+
+        def store(res, c, b, lo, n):
             h0 = HB * c + lo // DH
             nc.sync.dma_start(
                 out=out[h0 : h0 + n // DH, P * b : P * (b + 1), :].rearrange("h p d -> p h d"),
                 in_=res[:, 0:n].rearrange("p (h d) -> p h d", d=DH),
             )
 
-        items = []
-        for c in range(NC):
-            for b in range(NB):
-                first = c == 0 and b == 0
-                last = c == NC - 1 and b == NB - 1
-                if first or last:
-                    items.append((c, b, 0, CB // 2, last))
-                    items.append((c, b, CB // 2, CB, last))
+        def add_store(engine, prod, c, b, lo, hi):
+            n = hi - lo
+            res = work.tile([P, CB], F32, name="res", tag="res", bufs=8)
+            engine.tensor_tensor(
+                out=pairs(res[:, 0:n]),
+                in0=pairs(prod[:, 0, 0:n]),
+                in1=pairs(prod[:, 1, 0:n])[:, :, ::-1],
+                op=ALU.add,
+            )
+            store(res, c, b, lo, n)
+
+        def add_on_pe(prod, c, b):
+            total = psum.tile([P, CB], F32, name="acc", tag="acc")
+            for t in range(2):
+                nc.tensor.matmul(total[:], lhsT=ident[:], rhs=prod[:, t, :], start=(t == 0), stop=(t == 1))
+            res = work.tile([P, CB], F32, name="res", tag="res", bufs=8)
+            nc.scalar.copy(out=res[:], in_=total[:])
+            store(res, c, b, 0, CB)
+
+        LEAD = 6
+        steps = []
+        for i, modes in enumerate(MODES):
+            n = CB // len(modes)
+            for part, mode in enumerate(modes):
+                steps.append((i // NB, i % NB, n * part, n * part + n, mode))
+        accs = {}
+        pending = []
+        pair = []
+        for s in range(len(steps) + LEAD):
+            if s < len(steps):
+                c, b, lo, hi, mode = steps[s]
+                accs[s] = multiply(c, b, lo, hi)
+            while pending:
+                prod, c, b = pending.pop(0)
+                add_on_pe(prod, c, b)
+            d = s - LEAD
+            if d >= 0:
+                c, b, lo, hi, mode = steps[d]
+                acc = accs.pop(d)
+                if mode == "C":
+                    prod = work.tile([P, 2, CB], F32, name="prod", tag="prod", bufs=8)
+                    straight_product(prod, acc, b)
+                    rotated_product(nc.vector, prod, acc, b)
+                    pending.append((prod, c, b))
+                elif mode in "AB":
+                    if mode == "A":
+                        both = work.tile([P, 2, 2 * CB], F32, name="both", tag="both", bufs=3)
+                    products(acc, b, CB, both[:, :, CB * len(pair) : CB * len(pair) + CB])
+                    pair.append((c, b))
+                    if mode == "B":
+                        res2 = work.tile([P, 2 * CB], F32, name="res2", tag="res2", bufs=3)
+                        nc.gpsimd.tensor_tensor(
+                            out=pairs(res2[:]), in0=pairs(both[:, 0, :]), in1=pairs(both[:, 1, :])[:, :, ::-1], op=ALU.add
+                        )
+                        for half, (c, b) in enumerate(pair):
+                            store(res2[:, CB * half : CB * half + CB], c, b, 0, CB)
+                        pair.clear()
                 else:
-                    items.append((c, b, 0, CB, False))
-        for c, b, lo, hi, on_vector in items:
-            acc = multiply(c, b, lo, hi)
-            prod = products(acc, b, hi - lo)
-            add_store(nc.vector if on_vector else nc.gpsimd, prod, c, b, lo, hi)
+                    prod = work.tile([P, 2, CB], F32, name="prod", tag="prod", bufs=8)
+                    products(acc, b, hi - lo, prod[:, :, 0 : hi - lo])
+                    add_store(nc.vector if mode == "V" else nc.gpsimd, prod, c, b, lo, hi)

import math
from contextlib import ExitStack

import concourse.mybir as mybir
from concourse.masks import make_identity

S, D, H, DH = 512, 1536, 16, 128
G = D // 512
ROPE_BASE = 10000.0
FLOPS = 2 * S * D * H * DH

F32 = mybir.dt.float32
BF16 = mybir.dt.bfloat16
I32 = mybir.dt.int32
U8 = mybir.dt.uint8
FP4 = mybir.dt.float4_e2m1fn_x4
ALU = mybir.AluOpType
SIN = mybir.ActivationFunctionType.Sin

P = 128
NB = S // P
CB = 512
NC = H * DH // CB
HB = CB // DH
J = DH // 2
TWO_PI = 2.0 * math.pi
WARM = 8
MODES = ["GG","G","G","G","G","G","A","B","A","B","A","B","C","G","G","VV"]


def tile_attention_pa_kernel(tc, x_words, x_scales, w_words, w_scales, out):
    nc = tc.nc
    with ExitStack() as ctx:
        keep = ctx.enter_context(tc.tile_pool(name="keep", bufs=1))
        work = ctx.enter_context(tc.tile_pool(name="work", bufs=1))
        psum = ctx.enter_context(tc.psum_pool(name="psum", bufs=8))
        ctx.enter_context(tc.manual_schedule())

        x0 = keep.tile([P, G, 2 * P], U8, align_bytes=64)
        xr = keep.tile([P, G, 2 * (S - P)], U8, align_bytes=64)
        xs = keep.tile([P, G, S], U8, align_bytes=64)
        w0 = [keep.tile([P, 2 * CB], U8, name="w0_%d" % g, align_bytes=64) for g in range(G)]
        wr = [keep.tile([P, G, 2 * CB], U8, name="w_%d" % c, align_bytes=64) for c in range(1, NC)]
        ws0 = keep.tile([P, G, CB], U8, align_bytes=64)
        wsr = keep.tile([P, G, (NC - 1) * CB], U8, align_bytes=64)

        zeros = keep.tile([P, CB], BF16, align_bytes=64)
        ident = keep.tile([P, P], F32, align_bytes=64)
        pos = keep.tile([P, NB], F32)
        freq = keep.tile([P, J], F32)
        dummy = keep.tile([P, 1], F32)
        dummy2 = keep.tile([P, 1], F32)
        coef = [keep.tile([P, 2, DH], F32, name="coef_%d" % b) for b in range(NB)]

        nc.vector.memset(xs[:].rearrange("p g n -> p (g n)").bitcast(I32), 0)
        nc.vector.memset(dummy[:], 0.0)
        nc.vector.memset(freq[:, 0:1], 1.0)
        nc.vector.memset(ws0[:].rearrange("p g n -> p (g n)").bitcast(I32), 0)
        nc.gpsimd.iota(pos[:], pattern=[[P, NB]], base=0, channel_multiplier=1, allow_small_or_imprecise_dtypes=True)
        nc.gpsimd.memset(zeros[:], 0.0)
        nc.gpsimd.memset(wsr[:].rearrange("p g n -> p (g n)").bitcast(I32), 0)
        make_identity(nc, ident[:])
        nc.scalar.activation(out=dummy2[:], in_=dummy[:], func=SIN)

        def load_codes(dst, src):
            nc.sync.dma_start(out=dst.bitcast(I32), in_=src.bitcast(I32))

        def load_scales(dst, src):
            for q in range(4):
                nc.sync.dma_start(
                    out=dst[32 * q : 32 * q + 4, :, :].bitcast(I32),
                    in_=src[:, 4 * q : 4 * q + 4, :].rearrange("g r n -> r g n").bitcast(I32),
                )

        load_codes(x0[:], x_words[:, :, 0 : 2 * P].rearrange("g p c -> p g c"))
        load_codes(w0[0][:], w_words[0, :, 0 : 2 * CB])
        load_scales(xs, x_scales)
        load_scales(ws0, w_scales[:, :, 0:CB])
        load_codes(w0[1][:], w_words[1, :, 0 : 2 * CB])
        load_codes(w0[2][:], w_words[2, :, 0 : 2 * CB])
        load_codes(xr[:], x_words[:, :, 2 * P :].rearrange("g p c -> p g c"))
        load_codes(wr[0][:], w_words[:, :, 2 * CB : 4 * CB].rearrange("g p c -> p g c"))
        load_scales(wsr, w_scales[:, :, CB:])
        load_codes(wr[1][:], w_words[:, :, 4 * CB : 6 * CB].rearrange("g p c -> p g c"))
        load_codes(wr[2][:], w_words[:, :, 6 * CB : 8 * CB].rearrange("g p c -> p g c"))

        warm = psum.tile([P, CB], F32, name="acc", tag="acc")
        for i in range(WARM):
            nc.tensor.matmul(warm[:], lhsT=zeros[:, 0:P], rhs=zeros[:], start=True, stop=True)

        n = 1
        while n < J:
            nc.vector.tensor_scalar_mul(freq[:, n : 2 * n], freq[:, 0:n], ROPE_BASE ** (-n / J))
            n *= 2

        def tables(b0, b1):
            m = b1 - b0
            turns = keep.tile([P, 2, m, J], F32, name="turns_%d" % b0)
            whole = keep.tile([P, 2, m, J], I32, name="whole_%d" % b0)
            frac = keep.tile([P, 2, m, J], F32, name="frac_%d" % b0)
            for t, quarter in ((1, 0.0), (0, 0.25)):
                if t == 1:
                    nc.vector.scalar_tensor_tensor(
                        out=turns[:, 1, :, :],
                        in0=pos[:, b0:b1].unsqueeze(2).to_broadcast([P, m, J]),
                        scalar=1.0 / TWO_PI,
                        in1=freq[:].unsqueeze(1).to_broadcast([P, m, J]),
                        op0=ALU.mult,
                        op1=ALU.mult,
                    )
                else:
                    nc.vector.tensor_scalar_add(turns[:, 0, :, :], turns[:, 1, :, :], quarter)
            nc.vector.tensor_copy(out=whole[:], in_=turns[:])
            nc.vector.tensor_tensor(out=frac[:], in0=turns[:], in1=whole[:], op=ALU.subtract)
            for b in range(b0, b1):
                nc.scalar.activation(
                    out=coef[b][:, 0, :].rearrange("p (j e) -> p j e", e=2),
                    in_=frac[:, 0, b - b0, :].unsqueeze(2).to_broadcast([P, J, 2]),
                    func=SIN,
                    scale=TWO_PI,
                )
                for e in range(2):
                    nc.scalar.activation(
                        out=coef[b][:, 1, e::2],
                        in_=frac[:, 1, b - b0, :],
                        func=SIN,
                        scale=TWO_PI if e == 0 else -TWO_PI,
                    )

        tables(0, 1)
        tables(1, NB)

        def codes(c, b, g, lo, hi):
            if b == 0:
                lhs = x0[:, g, :]
            else:
                lhs = xr[:, g, 2 * P * (b - 1) : 2 * P * b]
            if c == 0:
                rhs, scale = w0[g][:, 2 * lo : 2 * hi], ws0[:, g, lo:hi]
            else:
                rhs = wr[c - 1][:, g, 2 * lo : 2 * hi]
                scale = wsr[:, g, CB * (c - 1) + lo : CB * (c - 1) + hi]
            return lhs.bitcast(FP4), xs[:, g, P * b : P * (b + 1)], rhs.bitcast(FP4), scale

        def multiply(c, b, lo, hi):
            acc = psum.tile([P, CB], F32, name="acc", tag="acc")
            for g in range(G):
                lhs, ls, rhs, rs = codes(c, b, g, lo, hi)
                nc.tensor.matmul_mx(
                    out=acc[:, 0 : hi - lo], lhsT=lhs, lhsT_scale=ls, rhs=rhs, rhs_scale=rs, start=(g == 0), stop=(g == G - 1)
                )
            return acc

        def pairs(ap):
            return ap.rearrange("p (j e) -> p j e", e=2)

        def products(acc, b, n, prod):
            h = n // DH
            nc.vector.tensor_tensor(
                out=prod.rearrange("p t (h c) -> p t h c", h=h),
                in0=acc[:, 0:n].rearrange("p (h c) -> p h c", h=h).unsqueeze(1).to_broadcast([P, 2, h, DH]),
                in1=coef[b][:].unsqueeze(2).to_broadcast([P, 2, h, DH]),
                op=ALU.mult,
            )

        def straight_product(prod, acc, b):
            nc.vector.tensor_tensor(
                out=prod[:, 0, :].rearrange("p (h c) -> p h c", h=HB),
                in0=acc[:].rearrange("p (h c) -> p h c", h=HB),
                in1=coef[b][:, 0, :].unsqueeze(1).to_broadcast([P, HB, DH]),
                op=ALU.mult,
            )

        def rotated_product(engine, prod, y, b):
            engine.tensor_tensor(
                out=prod[:, 1, :].rearrange("p (h j e) -> p h j e", h=HB, e=2),
                in0=y[:].rearrange("p (h j e) -> p h j e", h=HB, e=2)[:, :, :, ::-1],
                in1=pairs(coef[b][:, 1, :])[:, :, ::-1].unsqueeze(1).to_broadcast([P, HB, J, 2]),
                op=ALU.mult,
            )

        def store(res, c, b, lo, n):
            h0 = HB * c + lo // DH
            nc.sync.dma_start(
                out=out[h0 : h0 + n // DH, P * b : P * (b + 1), :].rearrange("h p d -> p h d"),
                in_=res[:, 0:n].rearrange("p (h d) -> p h d", d=DH),
            )

        def add_store(engine, prod, c, b, lo, hi):
            n = hi - lo
            res = work.tile([P, CB], F32, name="res", tag="res", bufs=8)
            engine.tensor_tensor(
                out=pairs(res[:, 0:n]),
                in0=pairs(prod[:, 0, 0:n]),
                in1=pairs(prod[:, 1, 0:n])[:, :, ::-1],
                op=ALU.add,
            )
            store(res, c, b, lo, n)

        def add_on_pe(prod, c, b):
            total = psum.tile([P, CB], F32, name="acc", tag="acc")
            for t in range(2):
                nc.tensor.matmul(total[:], lhsT=ident[:], rhs=prod[:, t, :], start=(t == 0), stop=(t == 1))
            res = work.tile([P, CB], F32, name="res", tag="res", bufs=8)
            nc.scalar.copy(out=res[:], in_=total[:])
            store(res, c, b, 0, CB)

        LEAD = 6
        steps = []
        for i, modes in enumerate(MODES):
            n = CB // len(modes)
            for part, mode in enumerate(modes):
                steps.append((i // NB, i % NB, n * part, n * part + n, mode))
        accs = {}
        pending = []
        pair = []
        for s in range(len(steps) + LEAD):
            if s < len(steps):
                c, b, lo, hi, mode = steps[s]
                accs[s] = multiply(c, b, lo, hi)
            while pending:
                prod, c, b = pending.pop(0)
                add_on_pe(prod, c, b)
            d = s - LEAD
            if d >= 0:
                c, b, lo, hi, mode = steps[d]
                acc = accs.pop(d)
                if mode == "C":
                    prod = work.tile([P, 2, CB], F32, name="prod", tag="prod", bufs=8)
                    straight_product(prod, acc, b)
                    rotated_product(nc.vector, prod, acc, b)
                    pending.append((prod, c, b))
                elif mode in "AB":
                    if mode == "A":
                        both = work.tile([P, 2, 2 * CB], F32, name="both", tag="both", bufs=3)
                    products(acc, b, CB, both[:, :, CB * len(pair) : CB * len(pair) + CB])
                    pair.append((c, b))
                    if mode == "B":
                        res2 = work.tile([P, 2 * CB], F32, name="res2", tag="res2", bufs=3)
                        nc.gpsimd.tensor_tensor(
                            out=pairs(res2[:]), in0=pairs(both[:, 0, :]), in1=pairs(both[:, 1, :])[:, :, ::-1], op=ALU.add
                        )
                        for half, (c, b) in enumerate(pair):
                            store(res2[:, CB * half : CB * half + CB], c, b, 0, CB)
                        pair.clear()
                else:
                    prod = work.tile([P, 2, CB], F32, name="prod", tag="prod", bufs=8)
                    products(acc, b, hi - lo, prod[:, :, 0 : hi - lo])
                    add_store(nc.vector if mode == "V" else nc.gpsimd, prod, c, b, lo, hi)
